import numpy as np
import ml_dtypes


def mxq(x, axis, fmt="e4m3"):
    dtype, down = {"e4m3": (ml_dtypes.float8_e4m3fn, 7), "e5m2": (ml_dtypes.float8_e5m2, 14)}[fmt]
    v = np.moveaxis(np.asarray(x, np.float32).astype(ml_dtypes.bfloat16).astype(np.float64), axis, -1)
    blocks = v.reshape(v.shape[:-1] + (-1, 32))
    amax = np.abs(blocks).max(-1, keepdims=True)
    byte = np.maximum(np.where(amax > 0, np.frexp(amax)[1] - 1 + 127, 0) - down, 1)
    scale = np.exp2(byte - 127.0)
    codes = (blocks / scale).astype(np.float32).astype(dtype).astype(np.float64)
    return np.moveaxis((codes * scale).reshape(v.shape), -1, axis)


WIDE = False


def mx_kscale(k):
    if not WIDE:
        return np.ones(k)
    levels = np.array([10, -10, 5, -5, 0])
    a = np.random.permutation(np.resize(levels, k // 512 * 4)).reshape(k // 512, 4)
    idx = np.arange(k)
    return np.exp2(a[idx // 512, idx % 128 // 32])


BF16 = ml_dtypes.bfloat16


def bf(x):
    return np.asarray(x, np.float32).astype(BF16)


def f64(x):
    return np.asarray(x).astype(np.float64)


G, GI, GO, B = 32, 32, 4, 8192
K = G * GI
N = G * GO


def build_mask():
    mask = np.ones((N, K))
    for g in range(G):
        mask[g * GO:(g + 1) * GO, g * GI:(g + 1) * GI] = 0.0
    return mask


def setup_inputs():
    s = mx_kscale(K)
    bound = 1.0 / np.sqrt(K)
    W = np.random.uniform(-bound, bound, (N, K)) * build_mask()
    return {"data": bf(np.random.standard_normal((B, K)) * s),
            "W": bf(W / s[None, :]),
            "b": bf(np.random.standard_normal(N) * 0.3)}


def reference(data, W, b):
    return (mxq(f64(data), 1, "e4m3") @ mxq(f64(W), 1, "e4m3").T) + f64(b)

@@ -1,0 +1,169 @@
+from contextlib import ExitStack
+
+import concourse.mybir as mybir
+from concourse.masks import make_identity
+
+F32 = mybir.dt.float32
+BF16 = mybir.dt.bfloat16
+U32 = mybir.dt.uint32
+U8 = mybir.dt.uint8
+FP8X4 = mybir.dt.float8_e4m3fn_x4
+ADD = mybir.AluOpType.add
+
+P = 128
+ROWS = 8192
+K = 1024
+N_OUT = 128
+T_ALL = ROWS // P
+PASSES = K // 512
+FLOPS = 2 * ROWS * K * N_OUT
+
+LOADS = [4] * 16
+CHUNKS = [4] * 16
+STORES = [16, 16, 16, 4, 4, 4, 4]
+VEC_EVERY = 8
+
+
+def tile_groupfc_t_kernel(tc, data, W, b, out):
+    nc = tc.nc
+    data_v = data.rearrange("(p t) k -> p t k", t=T_ALL)
+    out_v = out.rearrange("(p t) n -> p t n", t=T_ALL)
+
+    with ExitStack() as ctx:
+        const = ctx.enter_context(tc.tile_pool(name="const", bufs=1))
+        xpool = ctx.enter_context(tc.tile_pool(name="xpool", bufs=1))
+        opool = ctx.enter_context(tc.tile_pool(name="opool", bufs=1))
+        gpool = ctx.enter_context(tc.tile_pool(name="gpool", bufs=3))
+        qpool = ctx.enter_context(tc.tile_pool(name="qpool", bufs=3))
+        psum_t = ctx.enter_context(tc.psum_pool(name="psum_t", bufs=6))
+        psum_o = ctx.enter_context(tc.psum_pool(name="psum_o", bufs=2))
+        ctx.enter_context(tc.manual_schedule())
+
+        w_sb = const.tile([P, K], BF16, name="w_sb")
+        nc.scalar.dma_start(out=w_sb[:], in_=W)
+        unit_src = []
+        t0 = 0
+        for i, cnt in enumerate(LOADS):
+            x_sb = xpool.tile([P, cnt, K], BF16, name="x%d" % i)
+            nc.sync.dma_start(out=x_sb[:], in_=data_v[:, t0 : t0 + cnt, :])
+            for j in range(cnt):
+                unit_src.append((x_sb, j))
+            t0 += cnt
+
+        unit_dst = []
+        store_of = []
+        t0 = 0
+        for i, cnt in enumerate(STORES):
+            o_sb = opool.tile([P, cnt, N_OUT], F32, name="o%d" % i)
+            for j in range(cnt):
+                unit_dst.append((o_sb, j))
+            store_of.append((o_sb, t0, cnt))
+            t0 += cnt
+
+        ident = const.tile([P, P], F32, name="ident")
+        make_identity(nc, ident[:])
+        bz = const.tile([P, N_OUT], BF16, name="bz")
+        nc.vector.memset(bz[:], 0.0)
+        ones = const.tile([P, P], BF16, name="ones")
+        nc.vector.memset(ones[:], 1.0)
+        nc.scalar.dma_start(out=bz[0:1, :], in_=b.rearrange("(o n) -> o n", o=1))
+
+        def transposes(src_f32, bank):
+            for j in range(4):
+                nc.tensor.transpose(bank[:, j, :], src_f32[:, P * j : P * (j + 1)], ident[:])
+
+        def copy_out(engine_copy, bank, grouped_f32):
+            engine_copy(
+                out=grouped_f32.rearrange("p (g r u) -> p g r u", g=PASSES, u=2),
+                in_=bank[:].rearrange("p (g u) r -> p g r u", g=PASSES, u=2),
+            )
+
+        w_bank = psum_t.tile([P, 4, P], F32, name="xt", tag="xt")
+        transposes(w_sb[:].bitcast(F32), w_bank)
+        w_grouped = const.tile([P, K], BF16, name="w_grouped", align_bytes=64)
+        copy_out(nc.scalar.copy, w_bank, w_grouped[:].bitcast(F32))
+        w_codes = const.tile([P, PASSES * N_OUT], U32, name="w_codes", align_bytes=64)
+        w_scales = const.tile([P, PASSES * N_OUT], U8, name="w_scales", align_bytes=64)
+        nc.vector.quantize_mx(out=w_codes[:].bitcast(FP8X4), scales=w_scales[:], in_=w_grouped[:])
+
+        b_bank = psum_o.tile([P, 4, N_OUT], F32, name="acc", tag="acc")
+        nc.tensor.matmul(b_bank[:, 0, :], lhsT=ones[:], rhs=bz[:], start=True, stop=True)
+        bias4 = const.tile([P, 4, N_OUT], F32, name="bias4")
+        nc.vector.tensor_copy(out=bias4[:], in_=b_bank[:, 0:1, :].to_broadcast([P, 4, N_OUT]))
+
+        n = len(CHUNKS)
+        first = [sum(CHUNKS[:c]) for c in range(n)]
+        banks = {}
+        grouped = {}
+        codes = {}
+        scales = {}
+        accs = {}
+        stores_done = [0]
+
+        def stage_t(c):
+            banks[c] = []
+            for i in range(CHUNKS[c]):
+                x_sb, j = unit_src[first[c] + i]
+                bank = psum_t.tile([P, 4, P], F32, name="xt", tag="xt")
+                transposes(x_sb[:, j, :].bitcast(F32), bank)
+                banks[c].append(bank)
+
+        def stage_c(c):
+            g = gpool.tile([P, 4 * K], BF16, name="grouped", tag="grouped", align_bytes=64)
+            grouped[c] = g
+            g32 = g[:].bitcast(F32)
+            for i in range(CHUNKS[c]):
+                u = first[c] + i
+                eng = nc.vector.tensor_copy if u % VEC_EVERY == VEC_EVERY - 1 else nc.scalar.copy
+                copy_out(eng, banks[c][i], g32[:, 512 * i : 512 * (i + 1)])
+
+        def stage_q(c):
+            w = CHUNKS[c] * PASSES * P
+            cd = qpool.tile([P, 4 * PASSES * P], U32, name="codes", tag="codes", align_bytes=64)
+            sc = qpool.tile([P, 4 * PASSES * P], U8, name="scales", tag="scales", align_bytes=64)
+            codes[c] = cd
+            scales[c] = sc
+            nc.vector.quantize_mx(
+                out=cd[:, 0:w].bitcast(FP8X4), scales=sc[:, 0:w], in_=grouped[c][:, 0 : 4 * w]
+            )
+
+        def stage_m(c):
+            acc = psum_o.tile([P, 4, N_OUT], F32, name="acc", tag="acc")
+            accs[c] = acc
+            for i in range(CHUNKS[c]):
+                for g in range(PASSES):
+                    lo = (i * PASSES + g) * P
+                    nc.tensor.matmul_mx(
+                        out=acc[:, i, :],
+                        lhsT=codes[c][:, lo : lo + P].bitcast(FP8X4),
+                        lhsT_scale=scales[c][:, lo : lo + P],
+                        rhs=w_codes[:, g * N_OUT : (g + 1) * N_OUT].bitcast(FP8X4),
+                        rhs_scale=w_scales[:, g * N_OUT : (g + 1) * N_OUT],
+                        start=(g == 0),
+                        stop=(g == PASSES - 1),
+                    )
+
+        def stage_a(c):
+            cnt = CHUNKS[c]
+            o_sb, j = unit_dst[first[c]]
+            nc.vector.tensor_tensor(
+                out=o_sb[:, j : j + cnt, :], in0=accs[c][:, 0:cnt, :], in1=bias4[:, 0:cnt, :], op=ADD
+            )
+            done = first[c] + cnt
+            while stores_done[0] < len(store_of):
+                s_sb, s0, scnt = store_of[stores_done[0]]
+                if s0 + scnt > done:
+                    break
+                nc.sync.dma_start(out=out_v[:, s0 : s0 + scnt, :], in_=s_sb[:])
+                stores_done[0] += 1
+
+        for s in range(n + 2):
+            if s < n:
+                stage_t(s)
+            if 0 <= s - 1 < n:
+                stage_q(s - 1)
+            if s < n:
+                stage_c(s)
+            if 0 <= s - 2 < n:
+                stage_m(s - 2)
+                stage_a(s - 2)

@@ -18,10 +18,12 @@ T_ALL = ROWS // P
 PASSES = K // 512
 FLOPS = 2 * ROWS * K * N_OUT
 
-LOADS = [4] * 16
-CHUNKS = [4] * 16
+GROUP = 4
+GROUPS = [[1, 1, 2]] + [[4]] * 14 + [[2, 1, 1]]
 STORES = [16, 16, 16, 4, 4, 4, 4]
 VEC_EVERY = 8
+VEC_UNTIL = 56
+LAG = 2
 
 
 def tile_groupfc_t_kernel(tc, data, W, b, out):
@@ -43,18 +45,19 @@ def tile_groupfc_t_kernel(tc, data, W, b, out):
         nc.scalar.dma_start(out=w_sb[:], in_=W)
         unit_src = []
         t0 = 0
-        for i, cnt in enumerate(LOADS):
-            x_sb = xpool.tile([P, cnt, K], BF16, name="x%d" % i)
-            nc.sync.dma_start(out=x_sb[:], in_=data_v[:, t0 : t0 + cnt, :])
-            for j in range(cnt):
-                unit_src.append((x_sb, j))
-            t0 += cnt
+        for grp in GROUPS:
+            for cnt in grp:
+                x_sb = xpool.tile([P, cnt, K], BF16, name="x%d" % t0)
+                nc.sync.dma_start(out=x_sb[:], in_=data_v[:, t0 : t0 + cnt, :])
+                for j in range(cnt):
+                    unit_src.append((x_sb, j))
+                t0 += cnt
 
         unit_dst = []
         store_of = []
         t0 = 0
-        for i, cnt in enumerate(STORES):
-            o_sb = opool.tile([P, cnt, N_OUT], F32, name="o%d" % i)
+        for cnt in STORES:
+            o_sb = opool.tile([P, cnt, N_OUT], F32, name="o%d" % t0)
             for j in range(cnt):
                 unit_dst.append((o_sb, j))
             store_of.append((o_sb, t0, cnt))
@@ -86,70 +89,58 @@ def tile_groupfc_t_kernel(tc, data, W, b, out):
         w_scales = const.tile([P, PASSES * N_OUT], U8, name="w_scales", align_bytes=64)
         nc.vector.quantize_mx(out=w_codes[:].bitcast(FP8X4), scales=w_scales[:], in_=w_grouped[:])
 
-        b_bank = psum_o.tile([P, 4, N_OUT], F32, name="acc", tag="acc")
+        b_bank = psum_o.tile([P, GROUP, N_OUT], F32, name="acc", tag="acc")
         nc.tensor.matmul(b_bank[:, 0, :], lhsT=ones[:], rhs=bz[:], start=True, stop=True)
-        bias4 = const.tile([P, 4, N_OUT], F32, name="bias4")
-        nc.vector.tensor_copy(out=bias4[:], in_=b_bank[:, 0:1, :].to_broadcast([P, 4, N_OUT]))
+        bias4 = const.tile([P, GROUP, N_OUT], F32, name="bias4")
+        nc.vector.tensor_copy(out=bias4[:], in_=b_bank[:, 0:1, :].to_broadcast([P, GROUP, N_OUT]))
 
-        n = len(CHUNKS)
-        first = [sum(CHUNKS[:c]) for c in range(n)]
-        banks = {}
+        ng = len(GROUPS)
         grouped = {}
         codes = {}
         scales = {}
-        accs = {}
         stores_done = [0]
+        WORDS = PASSES * P
 
-        def stage_t(c):
-            banks[c] = []
-            for i in range(CHUNKS[c]):
-                x_sb, j = unit_src[first[c] + i]
+        def open_group(g):
+            grouped[g] = gpool.tile([P, GROUP * K], BF16, name="grouped", tag="grouped", align_bytes=64)
+            codes[g] = qpool.tile([P, GROUP * WORDS], U32, name="codes", tag="codes", align_bytes=64)
+            scales[g] = qpool.tile([P, GROUP * WORDS], U8, name="scales", tag="scales", align_bytes=64)
+
+        def transpose_and_copy(g, off, cnt):
+            g32 = grouped[g][:].bitcast(F32)
+            for i in range(off, off + cnt):
+                u = g * GROUP + i
+                x_sb, j = unit_src[u]
                 bank = psum_t.tile([P, 4, P], F32, name="xt", tag="xt")
                 transposes(x_sb[:, j, :].bitcast(F32), bank)
-                banks[c].append(bank)
+                on_vector = u % VEC_EVERY == VEC_EVERY - 1 and u < VEC_UNTIL
+                eng = nc.vector.tensor_copy if on_vector else nc.scalar.copy
+                copy_out(eng, bank, g32[:, (K // 2) * i : (K // 2) * (i + 1)])
 
-        def stage_c(c):
-            g = gpool.tile([P, 4 * K], BF16, name="grouped", tag="grouped", align_bytes=64)
-            grouped[c] = g
-            g32 = g[:].bitcast(F32)
-            for i in range(CHUNKS[c]):
-                u = first[c] + i
-                eng = nc.vector.tensor_copy if u % VEC_EVERY == VEC_EVERY - 1 else nc.scalar.copy
-                copy_out(eng, banks[c][i], g32[:, 512 * i : 512 * (i + 1)])
-
-        def stage_q(c):
-            w = CHUNKS[c] * PASSES * P
-            cd = qpool.tile([P, 4 * PASSES * P], U32, name="codes", tag="codes", align_bytes=64)
-            sc = qpool.tile([P, 4 * PASSES * P], U8, name="scales", tag="scales", align_bytes=64)
-            codes[c] = cd
-            scales[c] = sc
+        def quantise(g, off, cnt):
             nc.vector.quantize_mx(
-                out=cd[:, 0:w].bitcast(FP8X4), scales=sc[:, 0:w], in_=grouped[c][:, 0 : 4 * w]
+                out=codes[g][:, WORDS * off : WORDS * (off + cnt)].bitcast(FP8X4),
+                scales=scales[g][:, WORDS * off : WORDS * (off + cnt)],
+                in_=grouped[g][:, K * off : K * (off + cnt)],
             )
 
-        def stage_m(c):
-            acc = psum_o.tile([P, 4, N_OUT], F32, name="acc", tag="acc")
-            accs[c] = acc
-            for i in range(CHUNKS[c]):
-                for g in range(PASSES):
-                    lo = (i * PASSES + g) * P
+        def multiply_and_add(g):
+            acc = psum_o.tile([P, GROUP, N_OUT], F32, name="acc", tag="acc")
+            for i in range(GROUP):
+                for h in range(PASSES):
+                    lo = (i * PASSES + h) * P
                     nc.tensor.matmul_mx(
                         out=acc[:, i, :],
-                        lhsT=codes[c][:, lo : lo + P].bitcast(FP8X4),
-                        lhsT_scale=scales[c][:, lo : lo + P],
-                        rhs=w_codes[:, g * N_OUT : (g + 1) * N_OUT].bitcast(FP8X4),
-                        rhs_scale=w_scales[:, g * N_OUT : (g + 1) * N_OUT],
-                        start=(g == 0),
-                        stop=(g == PASSES - 1),
+                        lhsT=codes[g][:, lo : lo + P].bitcast(FP8X4),
+                        lhsT_scale=scales[g][:, lo : lo + P],
+                        rhs=w_codes[:, h * N_OUT : (h + 1) * N_OUT].bitcast(FP8X4),
+                        rhs_scale=w_scales[:, h * N_OUT : (h + 1) * N_OUT],
+                        start=(h == 0),
+                        stop=(h == PASSES - 1),
                     )
-
-        def stage_a(c):
-            cnt = CHUNKS[c]
-            o_sb, j = unit_dst[first[c]]
-            nc.vector.tensor_tensor(
-                out=o_sb[:, j : j + cnt, :], in0=accs[c][:, 0:cnt, :], in1=bias4[:, 0:cnt, :], op=ADD
-            )
-            done = first[c] + cnt
+            o_sb, j = unit_dst[g * GROUP]
+            nc.vector.tensor_tensor(out=o_sb[:, j : j + GROUP, :], in0=acc[:], in1=bias4[:], op=ADD)
+            done = (g + 1) * GROUP
             while stores_done[0] < len(store_of):
                 s_sb, s0, scnt = store_of[stores_done[0]]
                 if s0 + scnt > done:
@@ -157,13 +148,18 @@ def tile_groupfc_t_kernel(tc, data, W, b, out):
                 nc.sync.dma_start(out=out_v[:, s0 : s0 + scnt, :], in_=s_sb[:])
                 stores_done[0] += 1
 
-        for s in range(n + 2):
-            if s < n:
-                stage_t(s)
-            if 0 <= s - 1 < n:
-                stage_q(s - 1)
-            if s < n:
-                stage_c(s)
-            if 0 <= s - 2 < n:
-                stage_m(s - 2)
-                stage_a(s - 2)
+        pending = []
+        for step in range(ng + LAG):
+            if step < ng:
+                open_group(step)
+                off = 0
+                for cnt in GROUPS[step]:
+                    if pending:
+                        quantise(*pending.pop())
+                    transpose_and_copy(step, off, cnt)
+                    pending.append((step, off, cnt))
+                    off += cnt
+            elif pending:
+                quantise(*pending.pop())
+            if step >= LAG:
+                multiply_and_add(step - LAG)

@@ -20,7 +20,8 @@ FLOPS = 2 * ROWS * K * N_OUT
 
 GROUP = 4
 GROUPS = [[1, 1, 2]] + [[4]] * 14 + [[2, 1, 1]]
-STORES = [16, 16, 16, 4, 4, 4, 4]
+LOADS = [1, 1, 2, 4] + [8] * 4 + [4] * 5 + [2, 1, 1]
+STORES = [32, 16, 8, 4, 4]
 VEC_EVERY = 8
 VEC_UNTIL = 56
 LAG = 2
@@ -45,13 +46,12 @@ def tile_groupfc_t_kernel(tc, data, W, b, out):
         nc.scalar.dma_start(out=w_sb[:], in_=W)
         unit_src = []
         t0 = 0
-        for grp in GROUPS:
-            for cnt in grp:
-                x_sb = xpool.tile([P, cnt, K], BF16, name="x%d" % t0)
-                nc.sync.dma_start(out=x_sb[:], in_=data_v[:, t0 : t0 + cnt, :])
-                for j in range(cnt):
-                    unit_src.append((x_sb, j))
-                t0 += cnt
+        for cnt in LOADS:
+            x_sb = xpool.tile([P, cnt, K], BF16, name="x%d" % t0)
+            nc.sync.dma_start(out=x_sb[:], in_=data_v[:, t0 : t0 + cnt, :])
+            for j in range(cnt):
+                unit_src.append((x_sb, j))
+            t0 += cnt
 
         unit_dst = []
         store_of = []

@@ -18,19 +18,16 @@ T_ALL = ROWS // P
 PASSES = K // 512
 FLOPS = 2 * ROWS * K * N_OUT
 
-GROUP = 4
-GROUPS = [[1, 1, 2]] + [[4]] * 14 + [[2, 1, 1]]
-LOADS = [1, 1, 2, 4] + [8] * 4 + [4] * 5 + [2, 1, 1]
-STORES = [32, 16, 8, 4, 4]
+LOADS = [4] * 16
+CHUNKS = [4] * 16
+STORES = [16, 16, 16, 4, 4, 4, 4]
 VEC_EVERY = 8
-VEC_UNTIL = 56
-LAG = 2
 
 
 def tile_groupfc_t_kernel(tc, data, W, b, out):
     nc = tc.nc
-    data_v = data.rearrange("(p t) k -> p t k", t=T_ALL)
-    out_v = out.rearrange("(p t) n -> p t n", t=T_ALL)
+    data_v = data.rearrange("(c p j) k -> c p j k", p=P, j=4)
+    out_v = out.rearrange("(c p j) n -> p c (j n)", p=P, j=4)
 
     with ExitStack() as ctx:
         const = ctx.enter_context(tc.tile_pool(name="const", bufs=1))
@@ -46,9 +43,9 @@ def tile_groupfc_t_kernel(tc, data, W, b, out):
         nc.scalar.dma_start(out=w_sb[:], in_=W)
         unit_src = []
         t0 = 0
-        for cnt in LOADS:
-            x_sb = xpool.tile([P, cnt, K], BF16, name="x%d" % t0)
-            nc.sync.dma_start(out=x_sb[:], in_=data_v[:, t0 : t0 + cnt, :])
+        for i, cnt in enumerate(LOADS):
+            x_sb = xpool.tile([P, cnt, K], BF16, name="x%d" % i)
+            nc.sync.dma_start(out=x_sb[:], in_=data_v[i])
             for j in range(cnt):
                 unit_src.append((x_sb, j))
             t0 += cnt
@@ -56,8 +53,8 @@ def tile_groupfc_t_kernel(tc, data, W, b, out):
         unit_dst = []
         store_of = []
         t0 = 0
-        for cnt in STORES:
-            o_sb = opool.tile([P, cnt, N_OUT], F32, name="o%d" % t0)
+        for i, cnt in enumerate(STORES):
+            o_sb = opool.tile([P, cnt, N_OUT], F32, name="o%d" % i)
             for j in range(cnt):
                 unit_dst.append((o_sb, j))
             store_of.append((o_sb, t0, cnt))
@@ -89,77 +86,87 @@ def tile_groupfc_t_kernel(tc, data, W, b, out):
         w_scales = const.tile([P, PASSES * N_OUT], U8, name="w_scales", align_bytes=64)
         nc.vector.quantize_mx(out=w_codes[:].bitcast(FP8X4), scales=w_scales[:], in_=w_grouped[:])
 
-        b_bank = psum_o.tile([P, GROUP, N_OUT], F32, name="acc", tag="acc")
+        b_bank = psum_o.tile([P, 4, N_OUT], F32, name="acc", tag="acc")
         nc.tensor.matmul(b_bank[:, 0, :], lhsT=ones[:], rhs=bz[:], start=True, stop=True)
-        bias4 = const.tile([P, GROUP, N_OUT], F32, name="bias4")
-        nc.vector.tensor_copy(out=bias4[:], in_=b_bank[:, 0:1, :].to_broadcast([P, GROUP, N_OUT]))
+        bias4 = const.tile([P, 4, N_OUT], F32, name="bias4")
+        nc.vector.tensor_copy(out=bias4[:], in_=b_bank[:, 0:1, :].to_broadcast([P, 4, N_OUT]))
 
-        ng = len(GROUPS)
+        n = len(CHUNKS)
+        first = [sum(CHUNKS[:c]) for c in range(n)]
+        banks = {}
         grouped = {}
         codes = {}
         scales = {}
+        accs = {}
         stores_done = [0]
-        WORDS = PASSES * P
 
-        def open_group(g):
-            grouped[g] = gpool.tile([P, GROUP * K], BF16, name="grouped", tag="grouped", align_bytes=64)
-            codes[g] = qpool.tile([P, GROUP * WORDS], U32, name="codes", tag="codes", align_bytes=64)
-            scales[g] = qpool.tile([P, GROUP * WORDS], U8, name="scales", tag="scales", align_bytes=64)
-
-        def transpose_and_copy(g, off, cnt):
-            g32 = grouped[g][:].bitcast(F32)
-            for i in range(off, off + cnt):
-                u = g * GROUP + i
-                x_sb, j = unit_src[u]
+        def stage_t(c):
+            banks[c] = []
+            for i in range(CHUNKS[c]):
+                x_sb, j = unit_src[first[c] + i]
                 bank = psum_t.tile([P, 4, P], F32, name="xt", tag="xt")
                 transposes(x_sb[:, j, :].bitcast(F32), bank)
-                on_vector = u % VEC_EVERY == VEC_EVERY - 1 and u < VEC_UNTIL
-                eng = nc.vector.tensor_copy if on_vector else nc.scalar.copy
-                copy_out(eng, bank, g32[:, (K // 2) * i : (K // 2) * (i + 1)])
+                banks[c].append(bank)
 
-        def quantise(g, off, cnt):
+        def stage_c(c):
+            g = gpool.tile([P, 4 * K], BF16, name="grouped", tag="grouped", align_bytes=64)
+            grouped[c] = g
+            g32 = g[:].bitcast(F32)
+            for i in range(CHUNKS[c]):
+                u = first[c] + i
+                eng = nc.vector.tensor_copy if u % VEC_EVERY == VEC_EVERY - 1 else nc.scalar.copy
+                copy_out(eng, banks[c][i], g32[:, 512 * i : 512 * (i + 1)])
+
+        def stage_q(c):
+            w = CHUNKS[c] * PASSES * P
+            cd = qpool.tile([P, 4 * PASSES * P], U32, name="codes", tag="codes", align_bytes=64)
+            sc = qpool.tile([P, 4 * PASSES * P], U8, name="scales", tag="scales", align_bytes=64)
+            codes[c] = cd
+            scales[c] = sc
             nc.vector.quantize_mx(
-                out=codes[g][:, WORDS * off : WORDS * (off + cnt)].bitcast(FP8X4),
-                scales=scales[g][:, WORDS * off : WORDS * (off + cnt)],
-                in_=grouped[g][:, K * off : K * (off + cnt)],
+                out=cd[:, 0:w].bitcast(FP8X4), scales=sc[:, 0:w], in_=grouped[c][:, 0 : 4 * w]
             )
 
-        def multiply_and_add(g):
-            acc = psum_o.tile([P, GROUP, N_OUT], F32, name="acc", tag="acc")
-            for i in range(GROUP):
-                for h in range(PASSES):
-                    lo = (i * PASSES + h) * P
+        def stage_m(c):
+            acc = psum_o.tile([P, 4, N_OUT], F32, name="acc", tag="acc")
+            accs[c] = acc
+            for i in range(CHUNKS[c]):
+                for g in range(PASSES):
+                    lo = (i * PASSES + g) * P
                     nc.tensor.matmul_mx(
                         out=acc[:, i, :],
-                        lhsT=codes[g][:, lo : lo + P].bitcast(FP8X4),
-                        lhsT_scale=scales[g][:, lo : lo + P],
-                        rhs=w_codes[:, h * N_OUT : (h + 1) * N_OUT].bitcast(FP8X4),
-                        rhs_scale=w_scales[:, h * N_OUT : (h + 1) * N_OUT],
-                        start=(h == 0),
-                        stop=(h == PASSES - 1),
+                        lhsT=codes[c][:, lo : lo + P].bitcast(FP8X4),
+                        lhsT_scale=scales[c][:, lo : lo + P],
+                        rhs=w_codes[:, g * N_OUT : (g + 1) * N_OUT].bitcast(FP8X4),
+                        rhs_scale=w_scales[:, g * N_OUT : (g + 1) * N_OUT],
+                        start=(g == 0),
+                        stop=(g == PASSES - 1),
                     )
-            o_sb, j = unit_dst[g * GROUP]
-            nc.vector.tensor_tensor(out=o_sb[:, j : j + GROUP, :], in0=acc[:], in1=bias4[:], op=ADD)
-            done = (g + 1) * GROUP
+
+        def stage_a(c):
+            cnt = CHUNKS[c]
+            o_sb, j = unit_dst[first[c]]
+            nc.vector.tensor_tensor(
+                out=o_sb[:, j : j + cnt, :], in0=accs[c][:, 0:cnt, :], in1=bias4[:, 0:cnt, :], op=ADD
+            )
+            done = first[c] + cnt
             while stores_done[0] < len(store_of):
                 s_sb, s0, scnt = store_of[stores_done[0]]
                 if s0 + scnt > done:
                     break
-                nc.sync.dma_start(out=out_v[:, s0 : s0 + scnt, :], in_=s_sb[:])
+                nc.sync.dma_start(
+                    out=out_v[:, s0 // 4 : (s0 + scnt) // 4, :],
+                    in_=s_sb[:].rearrange("p (c j) n -> p c (j n)", j=4),
+                )
                 stores_done[0] += 1
 
-        pending = []
-        for step in range(ng + LAG):
-            if step < ng:
-                open_group(step)
-                off = 0
-                for cnt in GROUPS[step]:
-                    if pending:
-                        quantise(*pending.pop())
-                    transpose_and_copy(step, off, cnt)
-                    pending.append((step, off, cnt))
-                    off += cnt
-            elif pending:
-                quantise(*pending.pop())
-            if step >= LAG:
-                multiply_and_add(step - LAG)
+        for s in range(n + 2):
+            if s < n:
+                stage_t(s)
+            if 0 <= s - 1 < n:
+                stage_q(s - 1)
+            if s < n:
+                stage_c(s)
+            if 0 <= s - 2 < n:
+                stage_m(s - 2)
+                stage_a(s - 2)

from contextlib import ExitStack

import concourse.mybir as mybir
from concourse.masks import make_identity

F32 = mybir.dt.float32
BF16 = mybir.dt.bfloat16
U32 = mybir.dt.uint32
U8 = mybir.dt.uint8
FP8X4 = mybir.dt.float8_e4m3fn_x4
ADD = mybir.AluOpType.add

P = 128
ROWS = 8192
K = 1024
N_OUT = 128
T_ALL = ROWS // P
PASSES = K // 512
FLOPS = 2 * ROWS * K * N_OUT

LOADS = [4] * 16
CHUNKS = [4] * 16
STORES = [16, 16, 16, 4, 4, 4, 4]
VEC_EVERY = 8


def tile_groupfc_t_kernel(tc, data, W, b, out):
    nc = tc.nc
    data_v = data.rearrange("(c p j) k -> c p j k", p=P, j=4)
    out_v = out.rearrange("(c p j) n -> p c (j n)", p=P, j=4)

    with ExitStack() as ctx:
        const = ctx.enter_context(tc.tile_pool(name="const", bufs=1))
        xpool = ctx.enter_context(tc.tile_pool(name="xpool", bufs=1))
        opool = ctx.enter_context(tc.tile_pool(name="opool", bufs=1))
        gpool = ctx.enter_context(tc.tile_pool(name="gpool", bufs=3))
        qpool = ctx.enter_context(tc.tile_pool(name="qpool", bufs=3))
        psum_t = ctx.enter_context(tc.psum_pool(name="psum_t", bufs=6))
        psum_o = ctx.enter_context(tc.psum_pool(name="psum_o", bufs=2))
        ctx.enter_context(tc.manual_schedule())

        w_sb = const.tile([P, K], BF16, name="w_sb")
        nc.scalar.dma_start(out=w_sb[:], in_=W)
        unit_src = []
        t0 = 0
        for i, cnt in enumerate(LOADS):
            x_sb = xpool.tile([P, cnt, K], BF16, name="x%d" % i)
            nc.sync.dma_start(out=x_sb[:], in_=data_v[i])
            for j in range(cnt):
                unit_src.append((x_sb, j))
            t0 += cnt

        unit_dst = []
        store_of = []
        t0 = 0
        for i, cnt in enumerate(STORES):
            o_sb = opool.tile([P, cnt, N_OUT], F32, name="o%d" % i)
            for j in range(cnt):
                unit_dst.append((o_sb, j))
            store_of.append((o_sb, t0, cnt))
            t0 += cnt

        ident = const.tile([P, P], F32, name="ident")
        make_identity(nc, ident[:])
        bz = const.tile([P, N_OUT], BF16, name="bz")
        nc.vector.memset(bz[:], 0.0)
        ones = const.tile([P, P], BF16, name="ones")
        nc.vector.memset(ones[:], 1.0)
        nc.scalar.dma_start(out=bz[0:1, :], in_=b.rearrange("(o n) -> o n", o=1))

        def transposes(src_f32, bank):
            for j in range(4):
                nc.tensor.transpose(bank[:, j, :], src_f32[:, P * j : P * (j + 1)], ident[:])

        def copy_out(engine_copy, bank, grouped_f32):
            engine_copy(
                out=grouped_f32.rearrange("p (g r u) -> p g r u", g=PASSES, u=2),
                in_=bank[:].rearrange("p (g u) r -> p g r u", g=PASSES, u=2),
            )

        w_bank = psum_t.tile([P, 4, P], F32, name="xt", tag="xt")
        transposes(w_sb[:].bitcast(F32), w_bank)
        w_grouped = const.tile([P, K], BF16, name="w_grouped", align_bytes=64)
        copy_out(nc.scalar.copy, w_bank, w_grouped[:].bitcast(F32))
        w_codes = const.tile([P, PASSES * N_OUT], U32, name="w_codes", align_bytes=64)
        w_scales = const.tile([P, PASSES * N_OUT], U8, name="w_scales", align_bytes=64)
        nc.vector.quantize_mx(out=w_codes[:].bitcast(FP8X4), scales=w_scales[:], in_=w_grouped[:])

        b_bank = psum_o.tile([P, 4, N_OUT], F32, name="acc", tag="acc")
        nc.tensor.matmul(b_bank[:, 0, :], lhsT=ones[:], rhs=bz[:], start=True, stop=True)
        bias4 = const.tile([P, 4, N_OUT], F32, name="bias4")
        nc.vector.tensor_copy(out=bias4[:], in_=b_bank[:, 0:1, :].to_broadcast([P, 4, N_OUT]))

        n = len(CHUNKS)
        first = [sum(CHUNKS[:c]) for c in range(n)]
        banks = {}
        grouped = {}
        codes = {}
        scales = {}
        accs = {}
        stores_done = [0]

        def stage_t(c):
            banks[c] = []
            for i in range(CHUNKS[c]):
                x_sb, j = unit_src[first[c] + i]
                bank = psum_t.tile([P, 4, P], F32, name="xt", tag="xt")
                transposes(x_sb[:, j, :].bitcast(F32), bank)
                banks[c].append(bank)

        def stage_c(c):
            g = gpool.tile([P, 4 * K], BF16, name="grouped", tag="grouped", align_bytes=64)
            grouped[c] = g
            g32 = g[:].bitcast(F32)
            for i in range(CHUNKS[c]):
                u = first[c] + i
                eng = nc.vector.tensor_copy if u % VEC_EVERY == VEC_EVERY - 1 else nc.scalar.copy
                copy_out(eng, banks[c][i], g32[:, 512 * i : 512 * (i + 1)])

        def stage_q(c):
            w = CHUNKS[c] * PASSES * P
            cd = qpool.tile([P, 4 * PASSES * P], U32, name="codes", tag="codes", align_bytes=64)
            sc = qpool.tile([P, 4 * PASSES * P], U8, name="scales", tag="scales", align_bytes=64)
            codes[c] = cd
            scales[c] = sc
            nc.vector.quantize_mx(
                out=cd[:, 0:w].bitcast(FP8X4), scales=sc[:, 0:w], in_=grouped[c][:, 0 : 4 * w]
            )

        def stage_m(c):
            acc = psum_o.tile([P, 4, N_OUT], F32, name="acc", tag="acc")
            accs[c] = acc
            for i in range(CHUNKS[c]):
                for g in range(PASSES):
                    lo = (i * PASSES + g) * P
                    nc.tensor.matmul_mx(
                        out=acc[:, i, :],
                        lhsT=codes[c][:, lo : lo + P].bitcast(FP8X4),
                        lhsT_scale=scales[c][:, lo : lo + P],
                        rhs=w_codes[:, g * N_OUT : (g + 1) * N_OUT].bitcast(FP8X4),
                        rhs_scale=w_scales[:, g * N_OUT : (g + 1) * N_OUT],
                        start=(g == 0),
                        stop=(g == PASSES - 1),
                    )

        def stage_a(c):
            cnt = CHUNKS[c]
            o_sb, j = unit_dst[first[c]]
            nc.vector.tensor_tensor(
                out=o_sb[:, j : j + cnt, :], in0=accs[c][:, 0:cnt, :], in1=bias4[:, 0:cnt, :], op=ADD
            )
            done = first[c] + cnt
            while stores_done[0] < len(store_of):
                s_sb, s0, scnt = store_of[stores_done[0]]
                if s0 + scnt > done:
                    break
                nc.sync.dma_start(
                    out=out_v[:, s0 // 4 : (s0 + scnt) // 4, :],
                    in_=s_sb[:].rearrange("p (c j) n -> p c (j n)", j=4),
                )
                stores_done[0] += 1

        for s in range(n + 2):
            if s < n:
                stage_t(s)
            if 0 <= s - 1 < n:
                stage_q(s - 1)
            if s < n:
                stage_c(s)
            if 0 <= s - 2 < n:
                stage_m(s - 2)
                stage_a(s - 2)
